import numpy as np
import ml_dtypes


def mxq(x, axis, fmt="e4m3"):
    dtype, down = {"e4m3": (ml_dtypes.float8_e4m3fn, 7), "e5m2": (ml_dtypes.float8_e5m2, 14)}[fmt]
    v = np.moveaxis(np.asarray(x, np.float32).astype(ml_dtypes.bfloat16).astype(np.float64), axis, -1)
    blocks = v.reshape(v.shape[:-1] + (-1, 32))
    amax = np.abs(blocks).max(-1, keepdims=True)
    byte = np.maximum(np.where(amax > 0, np.frexp(amax)[1] - 1 + 127, 0) - down, 1)
    scale = np.exp2(byte - 127.0)
    codes = (blocks / scale).astype(np.float32).astype(dtype).astype(np.float64)
    return np.moveaxis((codes * scale).reshape(v.shape), -1, axis)


WIDE = False


def mx_kscale(k):
    if not WIDE:
        return np.ones(k)
    levels = np.array([10, -10, 5, -5, 0])
    a = np.random.permutation(np.resize(levels, k // 512 * 4)).reshape(k // 512, 4)
    idx = np.arange(k)
    return np.exp2(a[idx // 512, idx % 128 // 32])


BF16 = ml_dtypes.bfloat16


def bf(x):
    return np.asarray(x, np.float32).astype(BF16)


def f64(x):
    return np.asarray(x).astype(np.float64)


B, I, H = 4096, 512, 512
EPS = 1e-5


def sigmoid(v):
    return 1.0 / (1.0 + np.exp(-v))


def ln(v, g, b):
    m = v.mean(-1, keepdims=True)
    var = np.square(v - m).mean(-1, keepdims=True)
    return (v - m) / np.sqrt(var + EPS) * g + b


def setup_inputs():
    s, t = mx_kscale(I), mx_kscale(H)
    d = {"x": bf(np.random.standard_normal((B, I)) * s), "h": bf(np.random.standard_normal((B, H)) * t),
         "c": bf(np.random.standard_normal((B, H))), "ic_tilde": bf(0.35 * np.random.standard_normal((B, H)))}
    for g in ("f", "o"):
        d["W" + g + "_w"] = bf(np.random.standard_normal((H, I)) / np.sqrt(I) / s[None, :])
        d["W" + g + "_b"] = bf(np.random.standard_normal(H) * 0.5)
        d["U" + g + "_w"] = bf(np.random.standard_normal((H, H)) / np.sqrt(H) / t[None, :])
        d["ln" + g + "_g"] = bf(1.0 + 0.2 * np.random.standard_normal(H))
        d["ln" + g + "_b"] = bf(0.2 * np.random.standard_normal(H))
    return d


def reference(x, h, c, ic_tilde, Wf_w, Wf_b, Uf_w, lnf_g, lnf_b, Wo_w, Wo_b, Uo_w, lno_g, lno_b):
    xq = mxq(f64(x), 1, "e4m3")
    hq = mxq(f64(h), 1, "e4m3")
    pre_f = (xq @ mxq(f64(Wf_w), 1, "e4m3").T) + f64(Wf_b) + (hq @ mxq(f64(Uf_w), 1, "e4m3").T)
    pre_o = (xq @ mxq(f64(Wo_w), 1, "e4m3").T) + f64(Wo_b) + (hq @ mxq(f64(Uo_w), 1, "e4m3").T)
    f = sigmoid(ln(pre_f, f64(lnf_g), f64(lnf_b)))
    o = sigmoid(ln(pre_o, f64(lno_g), f64(lno_b)))
    c_new = f * f64(c) + f64(ic_tilde)
    h_new = o * np.tanh(c_new)
    return (h_new, c_new)

@@ -1,0 +1,293 @@
+from contextlib import ExitStack
+
+import concourse.mybir as mybir
+from concourse.masks import make_identity
+
+F32 = mybir.dt.float32
+BF16 = mybir.dt.bfloat16
+U32 = mybir.dt.uint32
+U8 = mybir.dt.uint8
+FP8X4 = mybir.dt.float8_e4m3fn_x4
+ALU = mybir.AluOpType
+ACT = mybir.ActivationFunctionType
+
+P = 128
+BATCH = 4096
+K = 512
+FEAT = 512
+WORDS = K // 2
+TILES = 2
+GROUPS = BATCH // (P * TILES)
+GATES = 2
+EPS = 1e-5
+
+FLOPS = 4 * 2 * BATCH * K * FEAT
+
+
+def tile_layernormlstmcell_pb_t_kernel(
+    tc, x, h, c, ic_tilde, Wf_w, Wf_b, Uf_w, lnf_g, lnf_b, Wo_w, Wo_b, Uo_w, lno_g, lno_b, out_0, out_1
+):
+    nc = tc.nc
+    with ExitStack() as ctx:
+        ctx.enter_context(tc.manual_schedule())
+        consts = ctx.enter_context(tc.tile_pool(name="consts", bufs=1))
+        wstage = ctx.enter_context(tc.tile_pool(name="wstage", bufs=2))
+        loads = ctx.enter_context(tc.tile_pool(name="loads", bufs=4))
+        mxin = ctx.enter_context(tc.tile_pool(name="mxin", bufs=2))
+        stats = ctx.enter_context(tc.tile_pool(name="stats", bufs=3))
+        acts = ctx.enter_context(tc.tile_pool(name="acts", bufs=5))
+        psum_keep = ctx.enter_context(tc.psum_pool(name="psum_keep", bufs=1))
+        psum = ctx.enter_context(tc.psum_pool(name="psum", bufs=2))
+
+        ident = consts.tile([P, P], F32)
+        make_identity(nc, ident[:])
+        ones = consts.tile([P, P], BF16)
+        nc.vector.memset(ones[:], 1.0)
+        neg_half = consts.tile([P, TILES * GATES], F32)
+        nc.vector.memset(neg_half[:], -0.5)
+        vec_rows = consts.tile([P, 6 * FEAT], BF16)
+        nc.vector.memset(vec_rows[:], 0.0)
+        warm = consts.tile([P, 1], F32)
+        nc.scalar.activation(out=warm[:], in_=neg_half[:, 0:1], func=ACT.Sigmoid)
+
+        w_codes = consts.tile([P, 4 * FEAT], U32, align_bytes=64)
+        w_scales = consts.tile([P, 4 * FEAT], U8, align_bytes=64)
+        raws = []
+        for w, weight in enumerate((Wf_w, Uf_w, Wo_w, Uo_w)):
+            raw = consts.tile([P, 4 * K], BF16, name="raw%d" % w)
+            nc.sync.dma_start(
+                out=raw[:].rearrange("p (b k) -> p b k", b=4),
+                in_=weight.rearrange("(b p) k -> p b k", p=P),
+            )
+            raws.append(raw)
+        for v, vec in enumerate((Wf_b, Wo_b, lnf_g, lnf_b, lno_g, lno_b)):
+            nc.sync.dma_start(out=vec_rows[0:1, v * FEAT : (v + 1) * FEAT], in_=vec.unsqueeze(0))
+        for w in range(4):
+            raw_words = raws[w][:].bitcast(F32)
+            grouped = wstage.tile([P, 4 * FEAT], BF16, align_bytes=64)
+            grouped_words = grouped[:].bitcast(F32).rearrange("p (j u) -> p j u", u=2)
+            for half in range(2):
+                turned = psum.tile([P, 2, 2 * P], F32, tag="turned")
+                for u in range(2):
+                    for b in range(2):
+                        first = (2 * half + b) * WORDS + u * P
+                        nc.tensor.transpose(
+                            out=turned[:, u, b * P : (b + 1) * P],
+                            in_=raw_words[:, first : first + P],
+                            identity=ident[:],
+                        )
+                copy = nc.scalar.copy if half == 0 else nc.vector.tensor_copy
+                copy(
+                    out=grouped_words[:, half * 2 * P : (half + 1) * 2 * P, :],
+                    in_=turned[:].rearrange("p u j -> p j u"),
+                )
+            nc.vector.quantize_mx(
+                out=w_codes[:, w * FEAT : (w + 1) * FEAT].bitcast(FP8X4),
+                scales=w_scales[:, w * FEAT : (w + 1) * FEAT],
+                in_=grouped[:],
+            )
+
+
+        def spread(dest, v):
+            nc.tensor.matmul(
+                out=dest, lhsT=ones[:], rhs=vec_rows[:, v * FEAT : (v + 1) * FEAT], start=True, stop=True
+            )
+
+        bias_ps = psum.tile([P, GATES * FEAT], BF16, tag="acc0")
+        bias = consts.tile([P, GATES * FEAT], BF16)
+        for gate in range(GATES):
+            spread(bias_ps[:, gate * FEAT : (gate + 1) * FEAT], gate)
+        nc.vector.tensor_copy(out=bias[:], in_=bias_ps[:])
+        gain_shift = []
+        for gate in range(GATES):
+            bank = psum_keep.tile([P, 2 * FEAT], BF16, name="gain_shift%d" % gate)
+            spread(bank[:, 0:FEAT], 2 + 2 * gate)
+            spread(bank[:, FEAT : 2 * FEAT], 3 + 2 * gate)
+            gain_shift.append(bank)
+
+        rows = "(g p t) k -> g p (t k)"
+        x_rows = x.rearrange(rows, p=P, t=TILES)
+        h_rows = h.rearrange(rows, p=P, t=TILES)
+        c_rows = c.rearrange(rows, p=P, t=TILES)
+        ic_rows = ic_tilde.rearrange(rows, p=P, t=TILES)
+        h_new_rows = out_0.rearrange(rows, p=P, t=TILES)
+        c_new_rows = out_1.rearrange(rows, p=P, t=TILES)
+        live = {}
+
+        def load_operands(g):
+            xh = loads.tile([P, 2 * TILES * K], BF16, name="xh")
+            nc.sync.dma_start(out=xh[:, 0 : TILES * K], in_=x_rows[g])
+            nc.sync.dma_start(out=xh[:, TILES * K : 2 * TILES * K], in_=h_rows[g])
+            live["xh", g] = xh
+
+        def load_cell(g):
+            c_old = loads.tile([P, TILES * FEAT], BF16, name="c_old")
+            ic = loads.tile([P, TILES * FEAT], BF16, name="ic")
+            nc.sync.dma_start(out=c_old[:], in_=c_rows[g])
+            nc.sync.dma_start(out=ic[:], in_=ic_rows[g])
+            live["c_old", g] = c_old
+            live["ic", g] = ic
+
+        def transpose_operands(g):
+            words = live["xh", g][:].bitcast(F32)
+            for t in range(TILES):
+                turned = psum.tile([P, 4, P], F32, tag="turned")
+                for operand in range(2):
+                    for u in range(2):
+                        first = (operand * TILES + t) * WORDS + u * P
+                        nc.tensor.transpose(
+                            out=turned[:, 2 * operand + u, :],
+                            in_=words[:, first : first + P],
+                            identity=ident[:],
+                        )
+                live["turned", g, t] = turned
+
+        def regroup_operands(g):
+            grouped = mxin.tile([P, TILES * 2 * P * 4], BF16, name="grouped", align_bytes=64)
+            grouped_words = grouped[:].bitcast(F32).rearrange(
+                "p (t o r u) -> p t o r u", t=TILES, o=2, u=2
+            )
+            for t in range(TILES):
+                nc.scalar.copy(
+                    out=grouped_words[:, t],
+                    in_=live["turned", g, t][:].rearrange("p (o u) r -> p o r u", o=2),
+                )
+            live["grouped", g] = grouped
+
+        def quantise_operands(g):
+            codes = mxin.tile([P, TILES * 2 * P], U32, name="codes", align_bytes=64)
+            scales = mxin.tile([P, TILES * 2 * P], U8, name="scales", align_bytes=64)
+            nc.vector.quantize_mx(out=codes[:].bitcast(FP8X4), scales=scales[:], in_=live["grouped", g][:])
+            live["codes", g] = codes
+            live["scales", g] = scales
+
+        def multiply(g):
+            codes, scales = live["codes", g], live["scales", g]
+            for t in range(TILES):
+                acc = [psum.tile([P, FEAT], F32, name="acc%d" % gate, tag="acc%d" % gate) for gate in range(GATES)]
+                for operand in range(2):
+                    r_cols = slice((2 * t + operand) * P, (2 * t + operand + 1) * P)
+                    for gate in range(GATES):
+                        w_cols = slice((2 * gate + operand) * FEAT, (2 * gate + operand + 1) * FEAT)
+                        nc.tensor.matmul_mx(
+                            out=acc[gate][:],
+                            lhsT=codes[:, r_cols].bitcast(FP8X4),
+                            lhsT_scale=scales[:, r_cols],
+                            rhs=w_codes[:, w_cols].bitcast(FP8X4),
+                            rhs_scale=w_scales[:, w_cols],
+                            start=(operand == 0),
+                            stop=(operand == 1),
+                        )
+                live["acc", g, t] = acc
+
+        def add_bias(g):
+            act = [acts.tile([P, TILES, FEAT], F32, name="act%d" % gate, tag="act%d" % gate) for gate in range(GATES)]
+            sums = stats.tile([P, TILES * GATES], F32, name="sums")
+            for t in range(TILES):
+                for gate in range(GATES):
+                    col = GATES * t + gate
+                    nc.vector.scalar_tensor_tensor(
+                        out=act[gate][:, t, :],
+                        in0=live["acc", g, t][gate][:],
+                        scalar=1.0,
+                        in1=bias[:, gate * FEAT : (gate + 1) * FEAT],
+                        op0=ALU.mult,
+                        op1=ALU.add,
+                        accum_out=sums[:, col : col + 1],
+                    )
+            live["act", g] = act
+            live["sums", g] = sums
+
+        def deviations(g):
+            act = live["act", g]
+            neg_mean = stats.tile([P, TILES * GATES], F32, name="neg_mean")
+            sq_dev = stats.tile([P, TILES * GATES], F32, name="sq_dev")
+            for t in range(TILES):
+                cols = slice(GATES * t, GATES * (t + 1))
+                nc.scalar.mul(out=neg_mean[:, cols], in_=live["sums", g][:, cols], mul=-1.0 / FEAT)
+                for gate in range(GATES):
+                    col = GATES * t + gate
+                    squares = acts.tile([P, FEAT], F32, name="squares")
+                    nc.scalar.activation(
+                        out=squares[:],
+                        in_=act[gate][:, t, :],
+                        func=ACT.Square,
+                        bias=neg_mean[:, col : col + 1],
+                        scale=1.0,
+                        accum_out=sq_dev[:, col : col + 1],
+                    )
+            live["neg_mean", g] = neg_mean
+            live["sq_dev", g] = sq_dev
+
+        def centre_and_gain(g):
+            for t in range(TILES):
+                for gate in range(GATES):
+                    col = GATES * t + gate
+                    nc.vector.scalar_tensor_tensor(
+                        out=live["act", g][gate][:, t, :],
+                        in0=live["act", g][gate][:, t, :],
+                        scalar=live["neg_mean", g][:, col : col + 1],
+                        in1=gain_shift[gate][:, 0:FEAT],
+                        op0=ALU.add,
+                        op1=ALU.mult,
+                    )
+
+        def inverse_std(g):
+            var_eps = stats.tile([P, TILES * GATES], F32, name="var_eps")
+            rstd = stats.tile([P, TILES * GATES], F32, name="rstd")
+            nc.gpsimd.tensor_scalar(
+                out=var_eps[:], in0=live["sq_dev", g][:], scalar1=1.0 / FEAT, scalar2=EPS, op0=ALU.mult, op1=ALU.add
+            )
+            nc.gpsimd.tensor_tensor(out=rstd[:], in0=var_eps[:], in1=neg_half[:], op=ALU.pow)
+            live["rstd", g] = rstd
+
+        def scale_and_shift(g):
+            for gate in range(GATES):
+                for t in range(TILES):
+                    col = GATES * t + gate
+                    nc.vector.scalar_tensor_tensor(
+                        out=live["act", g][gate][:, t, :],
+                        in0=live["act", g][gate][:, t, :],
+                        scalar=live["rstd", g][:, col : col + 1],
+                        in1=gain_shift[gate][:, FEAT : 2 * FEAT],
+                        op0=ALU.mult,
+                        op1=ALU.add,
+                    )
+
+        def sigmoids(g):
+            for gate in range(GATES):
+                nc.scalar.activation(out=live["act", g][gate][:], in_=live["act", g][gate][:], func=ACT.Sigmoid)
+
+        def new_cell(g):
+            cell = live["act", g][0][:].rearrange("p t f -> p (t f)")
+            nc.gpsimd.tensor_tensor(out=cell, in0=cell, in1=live["c_old", g][:], op=ALU.mult)
+            nc.gpsimd.tensor_tensor(out=cell, in0=cell, in1=live["ic", g][:], op=ALU.add)
+            tanh_c = acts.tile([P, TILES * FEAT], F32, name="tanh_c")
+            nc.scalar.activation(out=tanh_c[:], in_=cell, func=ACT.Tanh)
+            nc.sync.dma_start(out=c_new_rows[g], in_=cell)
+            live["tanh_c", g] = tanh_c
+
+        def new_hidden(g):
+            hidden = live["act", g][1][:].rearrange("p t f -> p (t f)")
+            nc.gpsimd.tensor_tensor(out=hidden, in0=hidden, in1=live["tanh_c", g][:], op=ALU.mult)
+            nc.sync.dma_start(out=h_new_rows[g], in_=hidden)
+
+        def at(stage, g):
+            if 0 <= g < GROUPS:
+                stage(g)
+
+        for step in range(-3, GROUPS + 3):
+            at(load_operands, step + 3)
+            at(load_cell, step)
+            at(regroup_operands, step + 1)
+            at(transpose_operands, step + 2)
+            at(add_bias, step)
+            at(deviations, step)
+            at(quantise_operands, step + 1)
+            at(multiply, step + 1)
+            at(scale_and_shift, step - 1)
+            at(sigmoids, step - 1)
+            at(centre_and_gain, step)
+            at(new_cell, step - 2)
+            at(inverse_std, step)
+            at(new_hidden, step - 3)

@@ -20,6 +20,7 @@ TILES = 2
 GROUPS = BATCH // (P * TILES)
 GATES = 2
 EPS = 1e-5
+VECTOR_EVERY = 4
 
 FLOPS = 4 * 2 * BATCH * K * FEAT
 
@@ -45,6 +46,8 @@ def tile_layernormlstmcell_pb_t_kernel(
         nc.vector.memset(ones[:], 1.0)
         neg_half = consts.tile([P, TILES * GATES], F32)
         nc.vector.memset(neg_half[:], -0.5)
+        eps = consts.tile([P, 1], F32)
+        nc.vector.memset(eps[:], EPS)
         vec_rows = consts.tile([P, 6 * FEAT], BF16)
         nc.vector.memset(vec_rows[:], 0.0)
         warm = consts.tile([P, 1], F32)
@@ -216,8 +219,10 @@ def tile_layernormlstmcell_pb_t_kernel(
                         scale=1.0,
                         accum_out=sq_dev[:, col : col + 1],
                     )
+            var_eps = stats.tile([P, TILES * GATES], F32, name="var_eps")
+            nc.scalar.activation(out=var_eps[:], in_=sq_dev[:], func=ACT.Identity, bias=eps[:], scale=1.0 / FEAT)
             live["neg_mean", g] = neg_mean
-            live["sq_dev", g] = sq_dev
+            live["var_eps", g] = var_eps
 
         def centre_and_gain(g):
             for t in range(TILES):
@@ -233,12 +238,8 @@ def tile_layernormlstmcell_pb_t_kernel(
                     )
 
         def inverse_std(g):
-            var_eps = stats.tile([P, TILES * GATES], F32, name="var_eps")
             rstd = stats.tile([P, TILES * GATES], F32, name="rstd")
-            nc.gpsimd.tensor_scalar(
-                out=var_eps[:], in0=live["sq_dev", g][:], scalar1=1.0 / FEAT, scalar2=EPS, op0=ALU.mult, op1=ALU.add
-            )
-            nc.gpsimd.tensor_tensor(out=rstd[:], in0=var_eps[:], in1=neg_half[:], op=ALU.pow)
+            nc.gpsimd.tensor_tensor(out=rstd[:], in0=live["var_eps", g][:], in1=neg_half[:], op=ALU.pow)
             live["rstd", g] = rstd
 
         def scale_and_shift(g):
@@ -258,10 +259,13 @@ def tile_layernormlstmcell_pb_t_kernel(
             for gate in range(GATES):
                 nc.scalar.activation(out=live["act", g][gate][:], in_=live["act", g][gate][:], func=ACT.Sigmoid)
 
+        def updater(g):
+            return nc.vector if (GROUPS - 1 - g) % VECTOR_EVERY == 0 else nc.gpsimd
+
         def new_cell(g):
             cell = live["act", g][0][:].rearrange("p t f -> p (t f)")
-            nc.gpsimd.tensor_tensor(out=cell, in0=cell, in1=live["c_old", g][:], op=ALU.mult)
-            nc.gpsimd.tensor_tensor(out=cell, in0=cell, in1=live["ic", g][:], op=ALU.add)
+            updater(g).tensor_tensor(out=cell, in0=cell, in1=live["c_old", g][:], op=ALU.mult)
+            updater(g).tensor_tensor(out=cell, in0=cell, in1=live["ic", g][:], op=ALU.add)
             tanh_c = acts.tile([P, TILES * FEAT], F32, name="tanh_c")
             nc.scalar.activation(out=tanh_c[:], in_=cell, func=ACT.Tanh)
             nc.sync.dma_start(out=c_new_rows[g], in_=cell)
@@ -269,7 +273,7 @@ def tile_layernormlstmcell_pb_t_kernel(
 
         def new_hidden(g):
             hidden = live["act", g][1][:].rearrange("p t f -> p (t f)")
-            nc.gpsimd.tensor_tensor(out=hidden, in0=hidden, in1=live["tanh_c", g][:], op=ALU.mult)
+            updater(g).tensor_tensor(out=hidden, in0=hidden, in1=live["tanh_c", g][:], op=ALU.mult)
             nc.sync.dma_start(out=h_new_rows[g], in_=hidden)
 
         def at(stage, g):

@@ -46,8 +46,6 @@ def tile_layernormlstmcell_pb_t_kernel(
         nc.vector.memset(ones[:], 1.0)
         neg_half = consts.tile([P, TILES * GATES], F32)
         nc.vector.memset(neg_half[:], -0.5)
-        eps = consts.tile([P, 1], F32)
-        nc.vector.memset(eps[:], EPS)
         vec_rows = consts.tile([P, 6 * FEAT], BF16)
         nc.vector.memset(vec_rows[:], 0.0)
         warm = consts.tile([P, 1], F32)
@@ -203,11 +201,8 @@ def tile_layernormlstmcell_pb_t_kernel(
 
         def deviations(g):
             act = live["act", g]
-            neg_mean = stats.tile([P, TILES * GATES], F32, name="neg_mean")
             sq_dev = stats.tile([P, TILES * GATES], F32, name="sq_dev")
             for t in range(TILES):
-                cols = slice(GATES * t, GATES * (t + 1))
-                nc.scalar.mul(out=neg_mean[:, cols], in_=live["sums", g][:, cols], mul=-1.0 / FEAT)
                 for gate in range(GATES):
                     col = GATES * t + gate
                     squares = acts.tile([P, FEAT], F32, name="squares")
@@ -215,14 +210,14 @@ def tile_layernormlstmcell_pb_t_kernel(
                         out=squares[:],
                         in_=act[gate][:, t, :],
                         func=ACT.Square,
-                        bias=neg_mean[:, col : col + 1],
-                        scale=1.0,
+                        bias=live["sums", g][:, col : col + 1],
+                        scale=-1.0 * FEAT,
                         accum_out=sq_dev[:, col : col + 1],
                     )
-            var_eps = stats.tile([P, TILES * GATES], F32, name="var_eps")
-            nc.scalar.activation(out=var_eps[:], in_=sq_dev[:], func=ACT.Identity, bias=eps[:], scale=1.0 / FEAT)
+            neg_mean = stats.tile([P, TILES * GATES], F32, name="neg_mean")
+            nc.scalar.mul(out=neg_mean[:], in_=live["sums", g][:], mul=-1.0 / FEAT)
             live["neg_mean", g] = neg_mean
-            live["var_eps", g] = var_eps
+            live["sq_dev", g] = sq_dev
 
         def centre_and_gain(g):
             for t in range(TILES):
@@ -238,8 +233,12 @@ def tile_layernormlstmcell_pb_t_kernel(
                     )
 
         def inverse_std(g):
+            var_eps = stats.tile([P, TILES * GATES], F32, name="var_eps")
             rstd = stats.tile([P, TILES * GATES], F32, name="rstd")
-            nc.gpsimd.tensor_tensor(out=rstd[:], in0=live["var_eps", g][:], in1=neg_half[:], op=ALU.pow)
+            nc.gpsimd.tensor_scalar(
+                out=var_eps[:], in0=live["sq_dev", g][:], scalar1=1.0 / FEAT**3, scalar2=EPS, op0=ALU.mult, op1=ALU.add
+            )
+            nc.gpsimd.tensor_tensor(out=rstd[:], in0=var_eps[:], in1=neg_half[:], op=ALU.pow)
             live["rstd", g] = rstd
 
         def scale_and_shift(g):

@@ -21,6 +21,9 @@ GROUPS = BATCH // (P * TILES)
 GATES = 2
 EPS = 1e-5
 VECTOR_EVERY = 4
+QUANT_GROUPS = 2
+PAIRS = GROUPS // QUANT_GROUPS
+GROUP_WORDS = TILES * 2 * P
 
 FLOPS = 4 * 2 * BATCH * K * FEAT
 
@@ -33,6 +36,7 @@ def tile_layernormlstmcell_pb_t_kernel(
         ctx.enter_context(tc.manual_schedule())
         consts = ctx.enter_context(tc.tile_pool(name="consts", bufs=1))
         wstage = ctx.enter_context(tc.tile_pool(name="wstage", bufs=2))
+        operands = ctx.enter_context(tc.tile_pool(name="operands", bufs=3 * QUANT_GROUPS))
         loads = ctx.enter_context(tc.tile_pool(name="loads", bufs=4))
         mxin = ctx.enter_context(tc.tile_pool(name="mxin", bufs=2))
         stats = ctx.enter_context(tc.tile_pool(name="stats", bufs=3))
@@ -53,6 +57,8 @@ def tile_layernormlstmcell_pb_t_kernel(
 
         w_codes = consts.tile([P, 4 * FEAT], U32, align_bytes=64)
         w_scales = consts.tile([P, 4 * FEAT], U8, align_bytes=64)
+        codes = consts.tile([P, GROUPS * GROUP_WORDS], U32, align_bytes=64)
+        scales = consts.tile([P, GROUPS * GROUP_WORDS], U8, align_bytes=64)
         raws = []
         for w, weight in enumerate((Wf_w, Uf_w, Wo_w, Uo_w)):
             raw = consts.tile([P, 4 * K], BF16, name="raw%d" % w)
@@ -116,7 +122,7 @@ def tile_layernormlstmcell_pb_t_kernel(
         live = {}
 
         def load_operands(g):
-            xh = loads.tile([P, 2 * TILES * K], BF16, name="xh")
+            xh = operands.tile([P, 2 * TILES * K], BF16, name="xh")
             nc.sync.dma_start(out=xh[:, 0 : TILES * K], in_=x_rows[g])
             nc.sync.dma_start(out=xh[:, TILES * K : 2 * TILES * K], in_=h_rows[g])
             live["xh", g] = xh
@@ -144,30 +150,41 @@ def tile_layernormlstmcell_pb_t_kernel(
                 live["turned", g, t] = turned
 
         def regroup_operands(g):
-            grouped = mxin.tile([P, TILES * 2 * P * 4], BF16, name="grouped", align_bytes=64)
-            grouped_words = grouped[:].bitcast(F32).rearrange(
-                "p (t o r u) -> p t o r u", t=TILES, o=2, u=2
+            pair, member = divmod(g, QUANT_GROUPS)
+            if member == 0:
+                live["grouped", pair] = mxin.tile(
+                    [P, QUANT_GROUPS * GROUP_WORDS * 4], BF16, name="grouped", align_bytes=64
+                )
+            grouped_words = live["grouped", pair][:].bitcast(F32).rearrange(
+                "p (m t o r u) -> p m t o r u", m=QUANT_GROUPS, t=TILES, o=2, u=2
             )
             for t in range(TILES):
                 nc.scalar.copy(
-                    out=grouped_words[:, t],
+                    out=grouped_words[:, member, t],
                     in_=live["turned", g, t][:].rearrange("p (o u) r -> p o r u", o=2),
                 )
-            live["grouped", g] = grouped
 
-        def quantise_operands(g):
-            codes = mxin.tile([P, TILES * 2 * P], U32, name="codes", align_bytes=64)
-            scales = mxin.tile([P, TILES * 2 * P], U8, name="scales", align_bytes=64)
-            nc.vector.quantize_mx(out=codes[:].bitcast(FP8X4), scales=scales[:], in_=live["grouped", g][:])
-            live["codes", g] = codes
-            live["scales", g] = scales
+        def load_pair(pair):
+            for g in range(pair * QUANT_GROUPS, (pair + 1) * QUANT_GROUPS):
+                load_operands(g)
+
+        def turn_pair(pair):
+            for g in range(pair * QUANT_GROUPS, (pair + 1) * QUANT_GROUPS):
+                transpose_operands(g)
+                regroup_operands(g)
+
+        def quantise_pair(pair):
+            cols = slice(pair * QUANT_GROUPS * GROUP_WORDS, (pair + 1) * QUANT_GROUPS * GROUP_WORDS)
+            nc.vector.quantize_mx(
+                out=codes[:, cols].bitcast(FP8X4), scales=scales[:, cols], in_=live["grouped", pair][:]
+            )
 
         def multiply(g):
-            codes, scales = live["codes", g], live["scales", g]
             for t in range(TILES):
                 acc = [psum.tile([P, FEAT], F32, name="acc%d" % gate, tag="acc%d" % gate) for gate in range(GATES)]
                 for operand in range(2):
-                    r_cols = slice((2 * t + operand) * P, (2 * t + operand + 1) * P)
+                    first = g * GROUP_WORDS + (2 * t + operand) * P
+                    r_cols = slice(first, first + P)
                     for gate in range(GATES):
                         w_cols = slice((2 * gate + operand) * FEAT, (2 * gate + operand + 1) * FEAT)
                         nc.tensor.matmul_mx(
@@ -275,22 +292,21 @@ def tile_layernormlstmcell_pb_t_kernel(
             updater(g).tensor_tensor(out=hidden, in0=hidden, in1=live["tanh_c", g][:], op=ALU.mult)
             nc.sync.dma_start(out=h_new_rows[g], in_=hidden)
 
-        def at(stage, g):
-            if 0 <= g < GROUPS:
-                stage(g)
+        def at(stage, i, count):
+            if 0 <= i < count:
+                stage(i)
 
-        for step in range(-3, GROUPS + 3):
-            at(load_operands, step + 3)
-            at(load_cell, step)
-            at(regroup_operands, step + 1)
-            at(transpose_operands, step + 2)
-            at(add_bias, step)
-            at(deviations, step)
-            at(quantise_operands, step + 1)
-            at(multiply, step + 1)
-            at(scale_and_shift, step - 1)
-            at(sigmoids, step - 1)
-            at(centre_and_gain, step)
-            at(new_cell, step - 2)
-            at(inverse_std, step)
-            at(new_hidden, step - 3)
+        for step in range(-4, GROUPS + 3):
+            at(load_pair, step + 4, PAIRS)
+            at(load_cell, step, GROUPS)
+            at(turn_pair, step + 2, PAIRS)
+            at(add_bias, step, GROUPS)
+            at(deviations, step, GROUPS)
+            at(multiply, step + 1, GROUPS)
+            at(scale_and_shift, step - 1, GROUPS)
+            at(sigmoids, step - 1, GROUPS)
+            at(quantise_pair, step + 2, PAIRS)
+            at(centre_and_gain, step, GROUPS)
+            at(new_cell, step - 2, GROUPS)
+            at(inverse_std, step, GROUPS)
+            at(new_hidden, step - 3, GROUPS)

from contextlib import ExitStack

import concourse.mybir as mybir
from concourse.masks import make_identity

F32 = mybir.dt.float32
BF16 = mybir.dt.bfloat16
U32 = mybir.dt.uint32
U8 = mybir.dt.uint8
FP8X4 = mybir.dt.float8_e4m3fn_x4
ALU = mybir.AluOpType
ACT = mybir.ActivationFunctionType

P = 128
BATCH = 4096
K = 512
FEAT = 512
WORDS = K // 2
TILES = 2
GROUPS = BATCH // (P * TILES)
GATES = 2
EPS = 1e-5
VECTOR_EVERY = 4
QUANT_GROUPS = 2
PAIRS = GROUPS // QUANT_GROUPS
GROUP_WORDS = TILES * 2 * P

FLOPS = 4 * 2 * BATCH * K * FEAT


def tile_layernormlstmcell_pb_t_kernel(
    tc, x, h, c, ic_tilde, Wf_w, Wf_b, Uf_w, lnf_g, lnf_b, Wo_w, Wo_b, Uo_w, lno_g, lno_b, out_0, out_1
):
    nc = tc.nc
    with ExitStack() as ctx:
        ctx.enter_context(tc.manual_schedule())
        consts = ctx.enter_context(tc.tile_pool(name="consts", bufs=1))
        wstage = ctx.enter_context(tc.tile_pool(name="wstage", bufs=2))
        operands = ctx.enter_context(tc.tile_pool(name="operands", bufs=3 * QUANT_GROUPS))
        loads = ctx.enter_context(tc.tile_pool(name="loads", bufs=4))
        mxin = ctx.enter_context(tc.tile_pool(name="mxin", bufs=2))
        stats = ctx.enter_context(tc.tile_pool(name="stats", bufs=3))
        acts = ctx.enter_context(tc.tile_pool(name="acts", bufs=5))
        psum_keep = ctx.enter_context(tc.psum_pool(name="psum_keep", bufs=1))
        psum = ctx.enter_context(tc.psum_pool(name="psum", bufs=2))

        ident = consts.tile([P, P], F32)
        make_identity(nc, ident[:])
        ones = consts.tile([P, P], BF16)
        nc.vector.memset(ones[:], 1.0)
        neg_half = consts.tile([P, TILES * GATES], F32)
        nc.vector.memset(neg_half[:], -0.5)
        vec_rows = consts.tile([P, 6 * FEAT], BF16)
        nc.vector.memset(vec_rows[:], 0.0)
        warm = consts.tile([P, 1], F32)
        nc.scalar.activation(out=warm[:], in_=neg_half[:, 0:1], func=ACT.Sigmoid)

        w_codes = consts.tile([P, 4 * FEAT], U32, align_bytes=64)
        w_scales = consts.tile([P, 4 * FEAT], U8, align_bytes=64)
        codes = consts.tile([P, GROUPS * GROUP_WORDS], U32, align_bytes=64)
        scales = consts.tile([P, GROUPS * GROUP_WORDS], U8, align_bytes=64)
        raws = []
        for w, weight in enumerate((Wf_w, Uf_w, Wo_w, Uo_w)):
            raw = consts.tile([P, 4 * K], BF16, name="raw%d" % w)
            nc.sync.dma_start(
                out=raw[:].rearrange("p (b k) -> p b k", b=4),
                in_=weight.rearrange("(b p) k -> p b k", p=P),
            )
            raws.append(raw)
        for v, vec in enumerate((Wf_b, Wo_b, lnf_g, lnf_b, lno_g, lno_b)):
            nc.sync.dma_start(out=vec_rows[0:1, v * FEAT : (v + 1) * FEAT], in_=vec.unsqueeze(0))
        for w in range(4):
            raw_words = raws[w][:].bitcast(F32)
            grouped = wstage.tile([P, 4 * FEAT], BF16, align_bytes=64)
            grouped_words = grouped[:].bitcast(F32).rearrange("p (j u) -> p j u", u=2)
            for half in range(2):
                turned = psum.tile([P, 2, 2 * P], F32, tag="turned")
                for u in range(2):
                    for b in range(2):
                        first = (2 * half + b) * WORDS + u * P
                        nc.tensor.transpose(
                            out=turned[:, u, b * P : (b + 1) * P],
                            in_=raw_words[:, first : first + P],
                            identity=ident[:],
                        )
                copy = nc.scalar.copy if half == 0 else nc.vector.tensor_copy
                copy(
                    out=grouped_words[:, half * 2 * P : (half + 1) * 2 * P, :],
                    in_=turned[:].rearrange("p u j -> p j u"),
                )
            nc.vector.quantize_mx(
                out=w_codes[:, w * FEAT : (w + 1) * FEAT].bitcast(FP8X4),
                scales=w_scales[:, w * FEAT : (w + 1) * FEAT],
                in_=grouped[:],
            )


        def spread(dest, v):
            nc.tensor.matmul(
                out=dest, lhsT=ones[:], rhs=vec_rows[:, v * FEAT : (v + 1) * FEAT], start=True, stop=True
            )

        bias_ps = psum.tile([P, GATES * FEAT], BF16, tag="acc0")
        bias = consts.tile([P, GATES * FEAT], BF16)
        for gate in range(GATES):
            spread(bias_ps[:, gate * FEAT : (gate + 1) * FEAT], gate)
        nc.vector.tensor_copy(out=bias[:], in_=bias_ps[:])
        gain_shift = []
        for gate in range(GATES):
            bank = psum_keep.tile([P, 2 * FEAT], BF16, name="gain_shift%d" % gate)
            spread(bank[:, 0:FEAT], 2 + 2 * gate)
            spread(bank[:, FEAT : 2 * FEAT], 3 + 2 * gate)
            gain_shift.append(bank)

        rows = "(g p t) k -> g p (t k)"
        x_rows = x.rearrange(rows, p=P, t=TILES)
        h_rows = h.rearrange(rows, p=P, t=TILES)
        c_rows = c.rearrange(rows, p=P, t=TILES)
        ic_rows = ic_tilde.rearrange(rows, p=P, t=TILES)
        h_new_rows = out_0.rearrange(rows, p=P, t=TILES)
        c_new_rows = out_1.rearrange(rows, p=P, t=TILES)
        live = {}

        def load_operands(g):
            xh = operands.tile([P, 2 * TILES * K], BF16, name="xh")
            nc.sync.dma_start(out=xh[:, 0 : TILES * K], in_=x_rows[g])
            nc.sync.dma_start(out=xh[:, TILES * K : 2 * TILES * K], in_=h_rows[g])
            live["xh", g] = xh

        def load_cell(g):
            c_old = loads.tile([P, TILES * FEAT], BF16, name="c_old")
            ic = loads.tile([P, TILES * FEAT], BF16, name="ic")
            nc.sync.dma_start(out=c_old[:], in_=c_rows[g])
            nc.sync.dma_start(out=ic[:], in_=ic_rows[g])
            live["c_old", g] = c_old
            live["ic", g] = ic

        def transpose_operands(g):
            words = live["xh", g][:].bitcast(F32)
            for t in range(TILES):
                turned = psum.tile([P, 4, P], F32, tag="turned")
                for operand in range(2):
                    for u in range(2):
                        first = (operand * TILES + t) * WORDS + u * P
                        nc.tensor.transpose(
                            out=turned[:, 2 * operand + u, :],
                            in_=words[:, first : first + P],
                            identity=ident[:],
                        )
                live["turned", g, t] = turned

        def regroup_operands(g):
            pair, member = divmod(g, QUANT_GROUPS)
            if member == 0:
                live["grouped", pair] = mxin.tile(
                    [P, QUANT_GROUPS * GROUP_WORDS * 4], BF16, name="grouped", align_bytes=64
                )
            grouped_words = live["grouped", pair][:].bitcast(F32).rearrange(
                "p (m t o r u) -> p m t o r u", m=QUANT_GROUPS, t=TILES, o=2, u=2
            )
            for t in range(TILES):
                nc.scalar.copy(
                    out=grouped_words[:, member, t],
                    in_=live["turned", g, t][:].rearrange("p (o u) r -> p o r u", o=2),
                )

        def load_pair(pair):
            for g in range(pair * QUANT_GROUPS, (pair + 1) * QUANT_GROUPS):
                load_operands(g)

        def turn_pair(pair):
            for g in range(pair * QUANT_GROUPS, (pair + 1) * QUANT_GROUPS):
                transpose_operands(g)
                regroup_operands(g)

        def quantise_pair(pair):
            cols = slice(pair * QUANT_GROUPS * GROUP_WORDS, (pair + 1) * QUANT_GROUPS * GROUP_WORDS)
            nc.vector.quantize_mx(
                out=codes[:, cols].bitcast(FP8X4), scales=scales[:, cols], in_=live["grouped", pair][:]
            )

        def multiply(g):
            for t in range(TILES):
                acc = [psum.tile([P, FEAT], F32, name="acc%d" % gate, tag="acc%d" % gate) for gate in range(GATES)]
                for operand in range(2):
                    first = g * GROUP_WORDS + (2 * t + operand) * P
                    r_cols = slice(first, first + P)
                    for gate in range(GATES):
                        w_cols = slice((2 * gate + operand) * FEAT, (2 * gate + operand + 1) * FEAT)
                        nc.tensor.matmul_mx(
                            out=acc[gate][:],
                            lhsT=codes[:, r_cols].bitcast(FP8X4),
                            lhsT_scale=scales[:, r_cols],
                            rhs=w_codes[:, w_cols].bitcast(FP8X4),
                            rhs_scale=w_scales[:, w_cols],
                            start=(operand == 0),
                            stop=(operand == 1),
                        )
                live["acc", g, t] = acc

        def add_bias(g):
            act = [acts.tile([P, TILES, FEAT], F32, name="act%d" % gate, tag="act%d" % gate) for gate in range(GATES)]
            sums = stats.tile([P, TILES * GATES], F32, name="sums")
            for t in range(TILES):
                for gate in range(GATES):
                    col = GATES * t + gate
                    nc.vector.scalar_tensor_tensor(
                        out=act[gate][:, t, :],
                        in0=live["acc", g, t][gate][:],
                        scalar=1.0,
                        in1=bias[:, gate * FEAT : (gate + 1) * FEAT],
                        op0=ALU.mult,
                        op1=ALU.add,
                        accum_out=sums[:, col : col + 1],
                    )
            live["act", g] = act
            live["sums", g] = sums

        def deviations(g):
            act = live["act", g]
            sq_dev = stats.tile([P, TILES * GATES], F32, name="sq_dev")
            for t in range(TILES):
                for gate in range(GATES):
                    col = GATES * t + gate
                    squares = acts.tile([P, FEAT], F32, name="squares")
                    nc.scalar.activation(
                        out=squares[:],
                        in_=act[gate][:, t, :],
                        func=ACT.Square,
                        bias=live["sums", g][:, col : col + 1],
                        scale=-1.0 * FEAT,
                        accum_out=sq_dev[:, col : col + 1],
                    )
            neg_mean = stats.tile([P, TILES * GATES], F32, name="neg_mean")
            nc.scalar.mul(out=neg_mean[:], in_=live["sums", g][:], mul=-1.0 / FEAT)
            live["neg_mean", g] = neg_mean
            live["sq_dev", g] = sq_dev

        def centre_and_gain(g):
            for t in range(TILES):
                for gate in range(GATES):
                    col = GATES * t + gate
                    nc.vector.scalar_tensor_tensor(
                        out=live["act", g][gate][:, t, :],
                        in0=live["act", g][gate][:, t, :],
                        scalar=live["neg_mean", g][:, col : col + 1],
                        in1=gain_shift[gate][:, 0:FEAT],
                        op0=ALU.add,
                        op1=ALU.mult,
                    )

        def inverse_std(g):
            var_eps = stats.tile([P, TILES * GATES], F32, name="var_eps")
            rstd = stats.tile([P, TILES * GATES], F32, name="rstd")
            nc.gpsimd.tensor_scalar(
                out=var_eps[:], in0=live["sq_dev", g][:], scalar1=1.0 / FEAT**3, scalar2=EPS, op0=ALU.mult, op1=ALU.add
            )
            nc.gpsimd.tensor_tensor(out=rstd[:], in0=var_eps[:], in1=neg_half[:], op=ALU.pow)
            live["rstd", g] = rstd

        def scale_and_shift(g):
            for gate in range(GATES):
                for t in range(TILES):
                    col = GATES * t + gate
                    nc.vector.scalar_tensor_tensor(
                        out=live["act", g][gate][:, t, :],
                        in0=live["act", g][gate][:, t, :],
                        scalar=live["rstd", g][:, col : col + 1],
                        in1=gain_shift[gate][:, FEAT : 2 * FEAT],
                        op0=ALU.mult,
                        op1=ALU.add,
                    )

        def sigmoids(g):
            for gate in range(GATES):
                nc.scalar.activation(out=live["act", g][gate][:], in_=live["act", g][gate][:], func=ACT.Sigmoid)

        def updater(g):
            return nc.vector if (GROUPS - 1 - g) % VECTOR_EVERY == 0 else nc.gpsimd

        def new_cell(g):
            cell = live["act", g][0][:].rearrange("p t f -> p (t f)")
            updater(g).tensor_tensor(out=cell, in0=cell, in1=live["c_old", g][:], op=ALU.mult)
            updater(g).tensor_tensor(out=cell, in0=cell, in1=live["ic", g][:], op=ALU.add)
            tanh_c = acts.tile([P, TILES * FEAT], F32, name="tanh_c")
            nc.scalar.activation(out=tanh_c[:], in_=cell, func=ACT.Tanh)
            nc.sync.dma_start(out=c_new_rows[g], in_=cell)
            live["tanh_c", g] = tanh_c

        def new_hidden(g):
            hidden = live["act", g][1][:].rearrange("p t f -> p (t f)")
            updater(g).tensor_tensor(out=hidden, in0=hidden, in1=live["tanh_c", g][:], op=ALU.mult)
            nc.sync.dma_start(out=h_new_rows[g], in_=hidden)

        def at(stage, i, count):
            if 0 <= i < count:
                stage(i)

        for step in range(-4, GROUPS + 3):
            at(load_pair, step + 4, PAIRS)
            at(load_cell, step, GROUPS)
            at(turn_pair, step + 2, PAIRS)
            at(add_bias, step, GROUPS)
            at(deviations, step, GROUPS)
            at(multiply, step + 1, GROUPS)
            at(scale_and_shift, step - 1, GROUPS)
            at(sigmoids, step - 1, GROUPS)
            at(quantise_pair, step + 2, PAIRS)
            at(centre_and_gain, step, GROUPS)
            at(new_cell, step - 2, GROUPS)
            at(inverse_std, step, GROUPS)
            at(new_hidden, step - 3, GROUPS)
